import numpy as np
import ml_dtypes


def mxq(x, axis, fmt="e4m3"):
    dtype, down = {"e4m3": (ml_dtypes.float8_e4m3fn, 7), "e5m2": (ml_dtypes.float8_e5m2, 14)}[fmt]
    v = np.moveaxis(np.asarray(x, np.float32).astype(ml_dtypes.bfloat16).astype(np.float64), axis, -1)
    blocks = v.reshape(v.shape[:-1] + (-1, 32))
    amax = np.abs(blocks).max(-1, keepdims=True)
    byte = np.maximum(np.where(amax > 0, np.frexp(amax)[1] - 1 + 127, 0) - down, 1)
    scale = np.exp2(byte - 127.0)
    codes = (blocks / scale).astype(np.float32).astype(dtype).astype(np.float64)
    return np.moveaxis((codes * scale).reshape(v.shape), -1, axis)


WIDE = False


def mx_kscale(k):
    if not WIDE:
        return np.ones(k)
    levels = np.array([10, -10, 5, -5, 0])
    a = np.random.permutation(np.resize(levels, k // 512 * 4)).reshape(k // 512, 4)
    idx = np.arange(k)
    return np.exp2(a[idx // 512, idx % 128 // 32])


BF16 = ml_dtypes.bfloat16


def bf(x):
    return np.asarray(x, np.float32).astype(BF16)


def f64(x):
    return np.asarray(x).astype(np.float64)


E2M1 = np.array([0.0, 0.5, 1.0, 1.5, 2.0, 3.0, 4.0, 6.0, -0.0, -0.5, -1.0, -1.5, -2.0, -3.0, -4.0, -6.0])


def pack_weight(w, fmt):
    k, n = w.shape
    w = f64(bf(w)).reshape(k // 32, 32, n)
    amax = np.abs(w).max(1)
    if fmt == "e4m3":
        byte = np.frexp(amax)[1] - 1 + 127 - 7
    else:
        mant, ex = np.frexp(amax / 6.0)
        byte = np.where(mant > 0.5, ex, ex - 1) + 127
    byte = np.clip(np.where(amax > 0, byte, 1), 1, 254)
    scaled = (w * np.exp2(127.0 - byte)[:, None, :]).reshape(k, n).astype(np.float32)
    by_word = np.ascontiguousarray(scaled.reshape(k // 512, 128, 4, n).transpose(0, 1, 3, 2))
    if fmt == "e4m3":
        words = by_word.astype(ml_dtypes.float8_e4m3fn).view(np.uint8)
    else:
        c = by_word.astype(ml_dtypes.float4_e2m1fn).view(np.uint8) & 0xF
        words = c[..., 0::2] | (c[..., 1::2] << 4)
    return np.ascontiguousarray(words), np.ascontiguousarray(byte.astype(np.uint8).reshape(k // 512, 16, n))


def unpack_weight(words, scales, fmt):
    g, p, n, _ = words.shape
    if fmt == "e4m3":
        vals = np.ascontiguousarray(words).view(ml_dtypes.float8_e4m3fn).astype(np.float64)
    else:
        nib = np.empty((g, p, n, 4), np.uint8)
        nib[..., 0::2] = words & 0xF
        nib[..., 1::2] = words >> 4
        vals = E2M1[nib]
    vals = vals * np.repeat(np.exp2(scales.astype(np.float64) - 127.0), 8, axis=1)[..., None]
    return vals.transpose(0, 1, 3, 2).reshape(g * 512, n)


B, S, K, N = 2, 128, 2048, 8192


def setup_inputs():
    s = mx_kscale(K)
    x = bf(np.random.standard_normal((B, S, K)) * s)
    w = np.random.standard_normal((K, N)) * 0.022 / s[:, None]
    w_words, w_scales = pack_weight(w, "e4m3")
    bias = bf(np.random.standard_normal(N))
    return {"x": x, "w_words": w_words, "w_scales": w_scales, "bias": bias}


def reference(x, w_words, w_scales, bias):
    w = unpack_weight(w_words, w_scales, "e4m3")
    return (mxq(f64(x), 2, "e4m3") @ w) + f64(bias)

@@ -1,0 +1,151 @@
+from contextlib import ExitStack
+
+import concourse.mybir as mybir
+from concourse.masks import make_identity
+
+F32 = mybir.dt.float32
+BF16 = mybir.dt.bfloat16
+I32 = mybir.dt.int32
+U8 = mybir.dt.uint8
+FP8X4 = mybir.dt.float8_e4m3fn_x4
+
+P = 128
+TOKENS = 256
+K = 2048
+N = 8192
+M_TILES = TOKENS // P
+PASSES = K // 512
+QUARTER = 2048
+N_QUARTERS = N // QUARTER
+BANK = 512
+BANKS_PER_QUARTER = QUARTER // BANK
+
+FLOPS = 2 * TOKENS * K * N
+
+
+def tile_quantizedlinear_kernel(tc, x, w_words, w_scales, bias, out):
+    nc = tc.nc
+    with ExitStack() as ctx:
+        ctx.enter_context(tc.manual_schedule())
+        keep = ctx.enter_context(tc.tile_pool(name="keep", bufs=1))
+        slabs = ctx.enter_context(tc.tile_pool(name="slabs", bufs=5))
+        psum = ctx.enter_context(tc.psum_pool(name="psum", bufs=8))
+
+        x_sb = keep.tile([P, M_TILES, K], BF16)
+        w_planes = keep.tile([P, N], U8, align_bytes=64)
+        bias_rows = keep.tile([P, BANK], BF16)
+        ident_f = keep.tile([P, P], F32)
+        ident_b = keep.tile([P, P], BF16)
+        grouped = keep.tile([P, M_TILES, PASSES, P, 4], BF16, align_bytes=64)
+        x_codes = keep.tile([P, M_TILES * PASSES, P], I32, align_bytes=64)
+        x_planes = keep.tile([P, M_TILES * PASSES, P], U8, align_bytes=64)
+        bias_bc = keep.tile([P, N], BF16)
+
+        nc.vector.memset(bias_rows[:], 0.0)
+        nc.vector.memset(w_planes[:].bitcast(I32), 0)
+        make_identity(nc, ident_b[:])
+        make_identity(nc, ident_f[:])
+
+        nc.sync.dma_start(out=x_sb[:], in_=x.rearrange("b s k -> s b k"))
+        nc.scalar.dma_start(
+            out=bias_rows[0 : N // BANK, :], in_=bias.rearrange("(r c) -> r c", c=BANK)
+        )
+        for quad in range(4):
+            nc.sync.dma_start(
+                out=w_planes[32 * quad : 32 * quad + 16, :].bitcast(I32),
+                in_=w_scales[:, 4 * quad : 4 * quad + 4, :].bitcast(I32),
+            )
+        w_tiles = []
+        for q in range(N_QUARTERS):
+            w_q = slabs.tile([P, PASSES, QUARTER], I32, tag="slab", name="w%d" % q, align_bytes=64)
+            w_tiles.append(w_q)
+            for g in range(PASSES):
+                nc.sync.dma_start(
+                    out=w_q[:, g, :],
+                    in_=w_words[g]
+                    .rearrange("p n t -> p (n t)")[:, 4 * QUARTER * q : 4 * QUARTER * (q + 1)]
+                    .bitcast(I32),
+                )
+
+        def spread_bias(j):
+            bank = psum.tile([P, BANK], F32, tag="bank", name="bb%d" % j)
+            nc.tensor.matmul(
+                bank[:],
+                lhsT=ident_b[:, j : j + 1].to_broadcast([P, P]),
+                rhs=bias_rows[:],
+                start=True,
+                stop=True,
+            )
+            nc.scalar.copy(out=bias_bc[:, BANK * j : BANK * (j + 1)], in_=bank[:])
+
+        for j in range(4):
+            spread_bias(j)
+
+        for m in range(M_TILES):
+            x_words = x_sb[:, m, :].bitcast(F32)
+            for half in range(2):
+                xt = psum.tile([P, 4, P], F32, tag="bank", name="xt%d%d" % (m, half))
+                for gi in range(2):
+                    g = 2 * half + gi
+                    for u in range(2):
+                        nc.tensor.transpose(
+                            xt[:, 2 * gi + u, :],
+                            x_words[:, 256 * g + u : 256 * (g + 1) : 2],
+                            ident_f[:],
+                        )
+                nc.vector.tensor_copy(
+                    out=grouped[:, m, 2 * half : 2 * half + 2].bitcast(F32),
+                    in_=xt[:].rearrange("p (g u) r -> p g r u", u=2),
+                )
+        for m in range(M_TILES):
+            nc.vector.quantize_mx(
+                out=x_codes[:, PASSES * m : PASSES * (m + 1), :]
+                .rearrange("p g r -> p (g r)")
+                .bitcast(FP8X4),
+                scales=x_planes[:, PASSES * m : PASSES * (m + 1), :].rearrange("p g r -> p (g r)"),
+                in_=grouped[:, m].rearrange("p g r t -> p (g r t)"),
+            )
+
+        for j in range(4, N // BANK):
+            spread_bias(j)
+
+        o_tiles = {}
+        for q in range(N_QUARTERS):
+            if q % 2 == 0:
+                o_tiles[q // 2] = slabs.tile(
+                    [P, 2, M_TILES, QUARTER], F32, tag="slab", name="o%d" % (q // 2), align_bytes=64
+                )
+            o_q = o_tiles[q // 2]
+            for j in range(BANKS_PER_QUARTER):
+                c0 = QUARTER * q + BANK * j
+                for m in range(M_TILES):
+                    acc = psum.tile([P, BANK], F32, tag="bank", name="acc%d_%d_%d" % (q, j, m))
+                    for g in range(PASSES):
+                        nc.tensor.matmul_mx(
+                            out=acc[:],
+                            lhsT=x_codes[:, PASSES * m + g, :].bitcast(FP8X4),
+                            lhsT_scale=x_planes[:, PASSES * m + g, :],
+                            rhs=w_tiles[q][:, g, BANK * j : BANK * (j + 1)].bitcast(FP8X4),
+                            rhs_scale=w_planes[4 * g : P, c0 : c0 + BANK],
+                            start=(g == 0),
+                            stop=(g == PASSES - 1),
+                        )
+                    nc.vector.tensor_tensor(
+                        out=o_q[:, q % 2, m, BANK * j : BANK * (j + 1)],
+                        in0=acc[:],
+                        in1=bias_bc[:, c0 : c0 + BANK],
+                        op=mybir.AluOpType.add,
+                    )
+                if q == N_QUARTERS - 1 and j % 2 == 1:
+                    lo = BANK * (j - 1)
+                    for m in range(M_TILES):
+                        nc.sync.dma_start(
+                            out=out[m, :, QUARTER * q + lo : QUARTER * q + lo + 2 * BANK],
+                            in_=o_q[:, q % 2, m, lo : lo + 2 * BANK],
+                        )
+            if q < N_QUARTERS - 1:
+                for m in range(M_TILES):
+                    nc.sync.dma_start(
+                        out=out[m, :, QUARTER * q : QUARTER * (q + 1)],
+                        in_=o_q[:, q % 2, m, :],
+                    )

@@ -51,9 +51,9 @@ def tile_quantizedlinear_kernel(tc, x, w_words, w_scales, bias, out):
             out=bias_rows[0 : N // BANK, :], in_=bias.rearrange("(r c) -> r c", c=BANK)
         )
         for quad in range(4):
-            nc.sync.dma_start(
-                out=w_planes[32 * quad : 32 * quad + 16, :].bitcast(I32),
-                in_=w_scales[:, 4 * quad : 4 * quad + 4, :].bitcast(I32),
+            nc.gpsimd.dma_start(
+                out=w_planes[32 * quad : 32 * quad + 16, :].bitcast(F32),
+                in_=w_scales[:, 4 * quad : 4 * quad + 4, :].bitcast(F32),
             )
         w_tiles = []
         for q in range(N_QUARTERS):

@@ -18,7 +18,8 @@ PASSES = K // 512
 QUARTER = 2048
 N_QUARTERS = N // QUARTER
 BANK = 512
-BANKS_PER_QUARTER = QUARTER // BANK
+HALF = QUARTER // 2
+LAG = 2
 
 FLOPS = 2 * TOKENS * K * N
 
@@ -51,9 +52,9 @@ def tile_quantizedlinear_kernel(tc, x, w_words, w_scales, bias, out):
             out=bias_rows[0 : N // BANK, :], in_=bias.rearrange("(r c) -> r c", c=BANK)
         )
         for quad in range(4):
-            nc.gpsimd.dma_start(
-                out=w_planes[32 * quad : 32 * quad + 16, :].bitcast(F32),
-                in_=w_scales[:, 4 * quad : 4 * quad + 4, :].bitcast(F32),
+            nc.sync.dma_start(
+                out=w_planes[32 * quad : 32 * quad + 16, :].bitcast(I32),
+                in_=w_scales[:, 4 * quad : 4 * quad + 4, :].bitcast(I32),
             )
         w_tiles = []
         for q in range(N_QUARTERS):
@@ -67,19 +68,21 @@ def tile_quantizedlinear_kernel(tc, x, w_words, w_scales, bias, out):
                     .bitcast(I32),
                 )
 
-        def spread_bias(j):
-            bank = psum.tile([P, BANK], F32, tag="bank", name="bb%d" % j)
-            nc.tensor.matmul(
-                bank[:],
-                lhsT=ident_b[:, j : j + 1].to_broadcast([P, P]),
-                rhs=bias_rows[:],
-                start=True,
-                stop=True,
-            )
-            nc.scalar.copy(out=bias_bc[:, BANK * j : BANK * (j + 1)], in_=bank[:])
+        def spread_bias(i):
+            bank = psum.tile([P, 2 * BANK], BF16, tag="bank", name="bb%d" % i)
+            for h in range(2):
+                j = 2 * i + h
+                nc.tensor.matmul(
+                    bank[:, BANK * h : BANK * (h + 1)],
+                    lhsT=ident_b[:, j : j + 1].to_broadcast([P, P]),
+                    rhs=bias_rows[:],
+                    start=True,
+                    stop=True,
+                )
+            nc.scalar.copy(out=bias_bc[:, 2 * BANK * i : 2 * BANK * (i + 1)], in_=bank[:])
 
-        for j in range(4):
-            spread_bias(j)
+        for i in range(3):
+            spread_bias(i)
 
         for m in range(M_TILES):
             x_words = x_sb[:, m, :].bitcast(F32)
@@ -106,46 +109,73 @@ def tile_quantizedlinear_kernel(tc, x, w_words, w_scales, bias, out):
                 in_=grouped[:, m].rearrange("p g r t -> p (g r t)"),
             )
 
-        for j in range(4, N // BANK):
-            spread_bias(j)
+        for i in range(3, N // (2 * BANK)):
+            spread_bias(i)
 
         o_tiles = {}
-        for q in range(N_QUARTERS):
-            if q % 2 == 0:
+        accs = {}
+
+        def open_set(q, half):
+            if half == 0 and q % 2 == 0:
                 o_tiles[q // 2] = slabs.tile(
                     [P, 2, M_TILES, QUARTER], F32, tag="slab", name="o%d" % (q // 2), align_bytes=64
                 )
+            for b in range(4):
+                accs[(q, half, b)] = psum.tile(
+                    [P, BANK], F32, tag="bank", name="acc%d_%d_%d" % (q, half, b)
+                )
+
+        def sweep(q, g, half):
+            for b in range(4):
+                jj, m = divmod(b, M_TILES)
+                lo = HALF * half + BANK * jj
+                c0 = QUARTER * q + lo
+                nc.tensor.matmul_mx(
+                    out=accs[(q, half, b)][:],
+                    lhsT=x_codes[:, PASSES * m + g, :].bitcast(FP8X4),
+                    lhsT_scale=x_planes[:, PASSES * m + g, :],
+                    rhs=w_tiles[q][:, g, lo : lo + BANK].bitcast(FP8X4),
+                    rhs_scale=w_planes[4 * g : P, c0 : c0 + BANK],
+                    start=(g == 0),
+                    stop=(g == PASSES - 1),
+                )
+
+        def drain_set(q, half):
             o_q = o_tiles[q // 2]
-            for j in range(BANKS_PER_QUARTER):
-                c0 = QUARTER * q + BANK * j
+            for b in range(4):
+                jj, m = divmod(b, M_TILES)
+                lo = HALF * half + BANK * jj
+                c0 = QUARTER * q + lo
+                nc.vector.tensor_tensor(
+                    out=o_q[:, q % 2, m, lo : lo + BANK],
+                    in0=accs[(q, half, b)][:],
+                    in1=bias_bc[:, c0 : c0 + BANK],
+                    op=mybir.AluOpType.add,
+                )
+            if q == N_QUARTERS - 1:
                 for m in range(M_TILES):
-                    acc = psum.tile([P, BANK], F32, tag="bank", name="acc%d_%d_%d" % (q, j, m))
-                    for g in range(PASSES):
-                        nc.tensor.matmul_mx(
-                            out=acc[:],
-                            lhsT=x_codes[:, PASSES * m + g, :].bitcast(FP8X4),
-                            lhsT_scale=x_planes[:, PASSES * m + g, :],
-                            rhs=w_tiles[q][:, g, BANK * j : BANK * (j + 1)].bitcast(FP8X4),
-                            rhs_scale=w_planes[4 * g : P, c0 : c0 + BANK],
-                            start=(g == 0),
-                            stop=(g == PASSES - 1),
-                        )
-                    nc.vector.tensor_tensor(
-                        out=o_q[:, q % 2, m, BANK * j : BANK * (j + 1)],
-                        in0=acc[:],
-                        in1=bias_bc[:, c0 : c0 + BANK],
-                        op=mybir.AluOpType.add,
+                    nc.sync.dma_start(
+                        out=out[m, :, QUARTER * q + HALF * half : QUARTER * q + HALF * (half + 1)],
+                        in_=o_q[:, q % 2, m, HALF * half : HALF * (half + 1)],
                     )
-                if q == N_QUARTERS - 1 and j % 2 == 1:
-                    lo = BANK * (j - 1)
-                    for m in range(M_TILES):
-                        nc.sync.dma_start(
-                            out=out[m, :, QUARTER * q + lo : QUARTER * q + lo + 2 * BANK],
-                            in_=o_q[:, q % 2, m, lo : lo + 2 * BANK],
-                        )
-            if q < N_QUARTERS - 1:
+            elif half == 1:
                 for m in range(M_TILES):
                     nc.sync.dma_start(
                         out=out[m, :, QUARTER * q : QUARTER * (q + 1)],
                         in_=o_q[:, q % 2, m, :],
                     )
+
+        def step(s, half):
+            q, g = divmod(s, PASSES)
+            if g == 0:
+                open_set(q, half)
+            sweep(q, g, half)
+            if g == PASSES - 1:
+                drain_set(q, half)
+
+        n_steps = N_QUARTERS * PASSES
+        for s in range(n_steps + LAG):
+            if s >= LAG:
+                step(s - LAG, 1)
+            if s < n_steps:
+                step(s, 0)

@@ -51,10 +51,10 @@ def tile_quantizedlinear_kernel(tc, x, w_words, w_scales, bias, out):
         nc.scalar.dma_start(
             out=bias_rows[0 : N // BANK, :], in_=bias.rearrange("(r c) -> r c", c=BANK)
         )
-        for quad in range(4):
-            nc.sync.dma_start(
-                out=w_planes[32 * quad : 32 * quad + 16, :].bitcast(I32),
-                in_=w_scales[:, 4 * quad : 4 * quad + 4, :].bitcast(I32),
+        for quad, odd in ((0, 0), (2, 0), (0, 1), (2, 1), (1, 0), (3, 0), (1, 1), (3, 1)):
+            nc.gpsimd.dma_start(
+                out=w_planes[32 * quad + odd : 32 * quad + 16 : 2, :].bitcast(F32),
+                in_=w_scales[:, 4 * quad + odd : 4 * quad + 4 : 2, :].bitcast(F32),
             )
         w_tiles = []
         for q in range(N_QUARTERS):

@@ -51,10 +51,15 @@ def tile_quantizedlinear_kernel(tc, x, w_words, w_scales, bias, out):
         nc.scalar.dma_start(
             out=bias_rows[0 : N // BANK, :], in_=bias.rearrange("(r c) -> r c", c=BANK)
         )
-        for quad, odd in ((0, 0), (2, 0), (0, 1), (2, 1), (1, 0), (3, 0), (1, 1), (3, 1)):
+        for quad in range(4):
+            nc.sync.dma_start(
+                out=w_planes[32 * quad : 32 * quad + 16, 0:QUARTER].bitcast(I32),
+                in_=w_scales[:, 4 * quad : 4 * quad + 4, 0:QUARTER].bitcast(I32),
+            )
+        for quad in range(4):
             nc.gpsimd.dma_start(
-                out=w_planes[32 * quad + odd : 32 * quad + 16 : 2, :].bitcast(F32),
-                in_=w_scales[:, 4 * quad + odd : 4 * quad + 4 : 2, :].bitcast(F32),
+                out=w_planes[32 * quad : 32 * quad + 16, QUARTER:N].bitcast(F32),
+                in_=w_scales[:, 4 * quad : 4 * quad + 4, QUARTER:N].bitcast(F32),
             )
         w_tiles = []
         for q in range(N_QUARTERS):

@@ -44,10 +44,11 @@ def tile_quantizedlinear_kernel(tc, x, w_words, w_scales, bias, out):
 
         nc.vector.memset(bias_rows[:], 0.0)
         nc.vector.memset(w_planes[:].bitcast(I32), 0)
-        make_identity(nc, ident_b[:])
         make_identity(nc, ident_f[:])
+        nc.vector.tensor_copy(out=ident_b[:], in_=ident_f[:])
 
-        nc.sync.dma_start(out=x_sb[:], in_=x.rearrange("b s k -> s b k"))
+        for m in range(M_TILES):
+            nc.sync.dma_start(out=x_sb[:, m, :], in_=x[m])
         nc.scalar.dma_start(
             out=bias_rows[0 : N // BANK, :], in_=bias.rearrange("(r c) -> r c", c=BANK)
         )
@@ -56,11 +57,12 @@ def tile_quantizedlinear_kernel(tc, x, w_words, w_scales, bias, out):
                 out=w_planes[32 * quad : 32 * quad + 16, 0:QUARTER].bitcast(I32),
                 in_=w_scales[:, 4 * quad : 4 * quad + 4, 0:QUARTER].bitcast(I32),
             )
-        for quad in range(4):
-            nc.gpsimd.dma_start(
-                out=w_planes[32 * quad : 32 * quad + 16, QUARTER:N].bitcast(F32),
-                in_=w_scales[:, 4 * quad : 4 * quad + 4, QUARTER:N].bitcast(F32),
-            )
+        for lo, hi in ((QUARTER, 3 * QUARTER), (3 * QUARTER, N)):
+            for quad in range(4):
+                nc.gpsimd.dma_start(
+                    out=w_planes[32 * quad : 32 * quad + 16, lo:hi].bitcast(F32),
+                    in_=w_scales[:, 4 * quad : 4 * quad + 4, lo:hi].bitcast(F32),
+                )
         w_tiles = []
         for q in range(N_QUARTERS):
             w_q = slabs.tile([P, PASSES, QUARTER], I32, tag="slab", name="w%d" % q, align_bytes=64)
@@ -86,26 +88,26 @@ def tile_quantizedlinear_kernel(tc, x, w_words, w_scales, bias, out):
                 )
             nc.scalar.copy(out=bias_bc[:, 2 * BANK * i : 2 * BANK * (i + 1)], in_=bank[:])
 
-        for i in range(3):
+        for i in range(2):
             spread_bias(i)
 
-        for m in range(M_TILES):
+        def transpose_half(m, half):
             x_words = x_sb[:, m, :].bitcast(F32)
-            for half in range(2):
-                xt = psum.tile([P, 4, P], F32, tag="bank", name="xt%d%d" % (m, half))
-                for gi in range(2):
-                    g = 2 * half + gi
-                    for u in range(2):
-                        nc.tensor.transpose(
-                            xt[:, 2 * gi + u, :],
-                            x_words[:, 256 * g + u : 256 * (g + 1) : 2],
-                            ident_f[:],
-                        )
-                nc.vector.tensor_copy(
-                    out=grouped[:, m, 2 * half : 2 * half + 2].bitcast(F32),
-                    in_=xt[:].rearrange("p (g u) r -> p g r u", u=2),
-                )
-        for m in range(M_TILES):
+            xt = psum.tile([P, 4, P], F32, tag="bank", name="xt%d%d" % (m, half))
+            for gi in range(2):
+                g = 2 * half + gi
+                for u in range(2):
+                    nc.tensor.transpose(
+                        xt[:, 2 * gi + u, :],
+                        x_words[:, 256 * g + u : 256 * (g + 1) : 2],
+                        ident_f[:],
+                    )
+            nc.vector.tensor_copy(
+                out=grouped[:, m, 2 * half : 2 * half + 2].bitcast(F32),
+                in_=xt[:].rearrange("p (g u) r -> p g r u", u=2),
+            )
+
+        def quantise(m):
             nc.vector.quantize_mx(
                 out=x_codes[:, PASSES * m : PASSES * (m + 1), :]
                 .rearrange("p g r -> p (g r)")
@@ -114,7 +116,14 @@ def tile_quantizedlinear_kernel(tc, x, w_words, w_scales, bias, out):
                 in_=grouped[:, m].rearrange("p g r t -> p (g r t)"),
             )
 
-        for i in range(3, N // (2 * BANK)):
+        transpose_half(0, 0)
+        transpose_half(0, 1)
+        transpose_half(1, 0)
+        quantise(0)
+        transpose_half(1, 1)
+        quantise(1)
+
+        for i in range(2, N // (2 * BANK)):
             spread_bias(i)
 
         o_tiles = {}

@@ -20,6 +20,7 @@ N_QUARTERS = N // QUARTER
 BANK = 512
 HALF = QUARTER // 2
 LAG = 2
+SCALE_ORDER = (2, 3, 0, 1)
 
 FLOPS = 2 * TOKENS * K * N
 
@@ -52,28 +53,11 @@ def tile_quantizedlinear_kernel(tc, x, w_words, w_scales, bias, out):
         nc.scalar.dma_start(
             out=bias_rows[0 : N // BANK, :], in_=bias.rearrange("(r c) -> r c", c=BANK)
         )
-        for quad in range(4):
+        for quad in SCALE_ORDER:
             nc.sync.dma_start(
-                out=w_planes[32 * quad : 32 * quad + 16, 0:QUARTER].bitcast(I32),
-                in_=w_scales[:, 4 * quad : 4 * quad + 4, 0:QUARTER].bitcast(I32),
+                out=w_planes[32 * quad : 32 * quad + 16, :].bitcast(I32),
+                in_=w_scales[:, 4 * quad : 4 * quad + 4, :].bitcast(I32),
             )
-        for lo, hi in ((QUARTER, 3 * QUARTER), (3 * QUARTER, N)):
-            for quad in range(4):
-                nc.gpsimd.dma_start(
-                    out=w_planes[32 * quad : 32 * quad + 16, lo:hi].bitcast(F32),
-                    in_=w_scales[:, 4 * quad : 4 * quad + 4, lo:hi].bitcast(F32),
-                )
-        w_tiles = []
-        for q in range(N_QUARTERS):
-            w_q = slabs.tile([P, PASSES, QUARTER], I32, tag="slab", name="w%d" % q, align_bytes=64)
-            w_tiles.append(w_q)
-            for g in range(PASSES):
-                nc.sync.dma_start(
-                    out=w_q[:, g, :],
-                    in_=w_words[g]
-                    .rearrange("p n t -> p (n t)")[:, 4 * QUARTER * q : 4 * QUARTER * (q + 1)]
-                    .bitcast(I32),
-                )
 
         def spread_bias(i):
             bank = psum.tile([P, 2 * BANK], BF16, tag="bank", name="bb%d" % i)
@@ -118,6 +102,25 @@ def tile_quantizedlinear_kernel(tc, x, w_words, w_scales, bias, out):
 
         transpose_half(0, 0)
         transpose_half(0, 1)
+
+        w_tiles = []
+        for q in range(N_QUARTERS):
+            w_q = slabs.tile([P, PASSES, QUARTER], I32, tag="slab", name="w%d" % q, align_bytes=64)
+            w_tiles.append(w_q)
+            if q == 0:
+                held = 32 * SCALE_ORDER[1]
+                nc.vector.tensor_copy(
+                    out=w_q[held : held + 16, 0, 0:1],
+                    in_=w_planes[held : held + 16, 0:4].bitcast(I32),
+                )
+            for g in range(PASSES):
+                nc.sync.dma_start(
+                    out=w_q[:, g, :],
+                    in_=w_words[g]
+                    .rearrange("p n t -> p (n t)")[:, 4 * QUARTER * q : 4 * QUARTER * (q + 1)]
+                    .bitcast(I32),
+                )
+
         transpose_half(1, 0)
         quantise(0)
         transpose_half(1, 1)

from contextlib import ExitStack

import concourse.mybir as mybir
from concourse.masks import make_identity

F32 = mybir.dt.float32
BF16 = mybir.dt.bfloat16
I32 = mybir.dt.int32
U8 = mybir.dt.uint8
FP8X4 = mybir.dt.float8_e4m3fn_x4

P = 128
TOKENS = 256
K = 2048
N = 8192
M_TILES = TOKENS // P
PASSES = K // 512
QUARTER = 2048
N_QUARTERS = N // QUARTER
BANK = 512
HALF = QUARTER // 2
LAG = 2
SCALE_ORDER = (2, 3, 0, 1)

FLOPS = 2 * TOKENS * K * N


def tile_quantizedlinear_kernel(tc, x, w_words, w_scales, bias, out):
    nc = tc.nc
    with ExitStack() as ctx:
        ctx.enter_context(tc.manual_schedule())
        keep = ctx.enter_context(tc.tile_pool(name="keep", bufs=1))
        slabs = ctx.enter_context(tc.tile_pool(name="slabs", bufs=5))
        psum = ctx.enter_context(tc.psum_pool(name="psum", bufs=8))

        x_sb = keep.tile([P, M_TILES, K], BF16)
        w_planes = keep.tile([P, N], U8, align_bytes=64)
        bias_rows = keep.tile([P, BANK], BF16)
        ident_f = keep.tile([P, P], F32)
        ident_b = keep.tile([P, P], BF16)
        grouped = keep.tile([P, M_TILES, PASSES, P, 4], BF16, align_bytes=64)
        x_codes = keep.tile([P, M_TILES * PASSES, P], I32, align_bytes=64)
        x_planes = keep.tile([P, M_TILES * PASSES, P], U8, align_bytes=64)
        bias_bc = keep.tile([P, N], BF16)

        nc.vector.memset(bias_rows[:], 0.0)
        nc.vector.memset(w_planes[:].bitcast(I32), 0)
        make_identity(nc, ident_f[:])
        nc.vector.tensor_copy(out=ident_b[:], in_=ident_f[:])

        for m in range(M_TILES):
            nc.sync.dma_start(out=x_sb[:, m, :], in_=x[m])
        nc.scalar.dma_start(
            out=bias_rows[0 : N // BANK, :], in_=bias.rearrange("(r c) -> r c", c=BANK)
        )
        for quad in SCALE_ORDER:
            nc.sync.dma_start(
                out=w_planes[32 * quad : 32 * quad + 16, :].bitcast(I32),
                in_=w_scales[:, 4 * quad : 4 * quad + 4, :].bitcast(I32),
            )

        def spread_bias(i):
            bank = psum.tile([P, 2 * BANK], BF16, tag="bank", name="bb%d" % i)
            for h in range(2):
                j = 2 * i + h
                nc.tensor.matmul(
                    bank[:, BANK * h : BANK * (h + 1)],
                    lhsT=ident_b[:, j : j + 1].to_broadcast([P, P]),
                    rhs=bias_rows[:],
                    start=True,
                    stop=True,
                )
            nc.scalar.copy(out=bias_bc[:, 2 * BANK * i : 2 * BANK * (i + 1)], in_=bank[:])

        for i in range(2):
            spread_bias(i)

        def transpose_half(m, half):
            x_words = x_sb[:, m, :].bitcast(F32)
            xt = psum.tile([P, 4, P], F32, tag="bank", name="xt%d%d" % (m, half))
            for gi in range(2):
                g = 2 * half + gi
                for u in range(2):
                    nc.tensor.transpose(
                        xt[:, 2 * gi + u, :],
                        x_words[:, 256 * g + u : 256 * (g + 1) : 2],
                        ident_f[:],
                    )
            nc.vector.tensor_copy(
                out=grouped[:, m, 2 * half : 2 * half + 2].bitcast(F32),
                in_=xt[:].rearrange("p (g u) r -> p g r u", u=2),
            )

        def quantise(m):
            nc.vector.quantize_mx(
                out=x_codes[:, PASSES * m : PASSES * (m + 1), :]
                .rearrange("p g r -> p (g r)")
                .bitcast(FP8X4),
                scales=x_planes[:, PASSES * m : PASSES * (m + 1), :].rearrange("p g r -> p (g r)"),
                in_=grouped[:, m].rearrange("p g r t -> p (g r t)"),
            )

        transpose_half(0, 0)
        transpose_half(0, 1)

        w_tiles = []
        for q in range(N_QUARTERS):
            w_q = slabs.tile([P, PASSES, QUARTER], I32, tag="slab", name="w%d" % q, align_bytes=64)
            w_tiles.append(w_q)
            if q == 0:
                held = 32 * SCALE_ORDER[1]
                nc.vector.tensor_copy(
                    out=w_q[held : held + 16, 0, 0:1],
                    in_=w_planes[held : held + 16, 0:4].bitcast(I32),
                )
            for g in range(PASSES):
                nc.sync.dma_start(
                    out=w_q[:, g, :],
                    in_=w_words[g]
                    .rearrange("p n t -> p (n t)")[:, 4 * QUARTER * q : 4 * QUARTER * (q + 1)]
                    .bitcast(I32),
                )

        transpose_half(1, 0)
        quantise(0)
        transpose_half(1, 1)
        quantise(1)

        for i in range(2, N // (2 * BANK)):
            spread_bias(i)

        o_tiles = {}
        accs = {}

        def open_set(q, half):
            if half == 0 and q % 2 == 0:
                o_tiles[q // 2] = slabs.tile(
                    [P, 2, M_TILES, QUARTER], F32, tag="slab", name="o%d" % (q // 2), align_bytes=64
                )
            for b in range(4):
                accs[(q, half, b)] = psum.tile(
                    [P, BANK], F32, tag="bank", name="acc%d_%d_%d" % (q, half, b)
                )

        def sweep(q, g, half):
            for b in range(4):
                jj, m = divmod(b, M_TILES)
                lo = HALF * half + BANK * jj
                c0 = QUARTER * q + lo
                nc.tensor.matmul_mx(
                    out=accs[(q, half, b)][:],
                    lhsT=x_codes[:, PASSES * m + g, :].bitcast(FP8X4),
                    lhsT_scale=x_planes[:, PASSES * m + g, :],
                    rhs=w_tiles[q][:, g, lo : lo + BANK].bitcast(FP8X4),
                    rhs_scale=w_planes[4 * g : P, c0 : c0 + BANK],
                    start=(g == 0),
                    stop=(g == PASSES - 1),
                )

        def drain_set(q, half):
            o_q = o_tiles[q // 2]
            for b in range(4):
                jj, m = divmod(b, M_TILES)
                lo = HALF * half + BANK * jj
                c0 = QUARTER * q + lo
                nc.vector.tensor_tensor(
                    out=o_q[:, q % 2, m, lo : lo + BANK],
                    in0=accs[(q, half, b)][:],
                    in1=bias_bc[:, c0 : c0 + BANK],
                    op=mybir.AluOpType.add,
                )
            if q == N_QUARTERS - 1:
                for m in range(M_TILES):
                    nc.sync.dma_start(
                        out=out[m, :, QUARTER * q + HALF * half : QUARTER * q + HALF * (half + 1)],
                        in_=o_q[:, q % 2, m, HALF * half : HALF * (half + 1)],
                    )
            elif half == 1:
                for m in range(M_TILES):
                    nc.sync.dma_start(
                        out=out[m, :, QUARTER * q : QUARTER * (q + 1)],
                        in_=o_q[:, q % 2, m, :],
                    )

        def step(s, half):
            q, g = divmod(s, PASSES)
            if g == 0:
                open_set(q, half)
            sweep(q, g, half)
            if g == PASSES - 1:
                drain_set(q, half)

        n_steps = N_QUARTERS * PASSES
        for s in range(n_steps + LAG):
            if s >= LAG:
                step(s - LAG, 1)
            if s < n_steps:
                step(s, 0)
